import numpy as np
import ml_dtypes


def mxq(x, axis, fmt="e4m3"):
    dtype, down = {"e4m3": (ml_dtypes.float8_e4m3fn, 7), "e5m2": (ml_dtypes.float8_e5m2, 14)}[fmt]
    v = np.moveaxis(np.asarray(x, np.float32).astype(ml_dtypes.bfloat16).astype(np.float64), axis, -1)
    blocks = v.reshape(v.shape[:-1] + (-1, 32))
    amax = np.abs(blocks).max(-1, keepdims=True)
    byte = np.maximum(np.where(amax > 0, np.frexp(amax)[1] - 1 + 127, 0) - down, 1)
    scale = np.exp2(byte - 127.0)
    codes = (blocks / scale).astype(np.float32).astype(dtype).astype(np.float64)
    return np.moveaxis((codes * scale).reshape(v.shape), -1, axis)


WIDE = False


def mx_kscale(k):
    if not WIDE:
        return np.ones(k)
    levels = np.array([10, -10, 5, -5, 0])
    a = np.random.permutation(np.resize(levels, k // 512 * 4)).reshape(k // 512, 4)
    idx = np.arange(k)
    return np.exp2(a[idx // 512, idx % 128 // 32])


BF16 = ml_dtypes.bfloat16


def bf(x):
    return np.asarray(x, np.float32).astype(BF16)


def f64(x):
    return np.asarray(x).astype(np.float64)


B, S, K, N = 4, 128, 2048, 5632


def setup_inputs():
    s = mx_kscale(K)
    return {"x": bf(np.random.standard_normal((B, S, K)) * s),
            "weight": bf(np.random.standard_normal((N, K)) * (1.0 / np.sqrt(K)) / s[None, :]),
            "wscales": bf(np.random.uniform(0.5, 1.5, (N, 1))),
            "bias": bf(np.random.standard_normal((1, N)) * 0.3)}


def reference(x, weight, wscales, bias):
    x2 = f64(x).reshape(-1, weight.shape[1])
    w_dequant = f64(weight) * f64(wscales)
    out = mxq(x2, 1, "e4m3") @ mxq(w_dequant, 1, "e4m3").T
    out = out.reshape(*x.shape[:-1], weight.shape[0])
    out = out + f64(bias)
    return out

@@ -1,0 +1,221 @@
+from contextlib import ExitStack
+
+import concourse.mybir as mybir
+from concourse.masks import make_identity
+
+FP8X4 = mybir.dt.float8_e4m3fn_x4
+BF16 = mybir.dt.bfloat16
+F32 = mybir.dt.float32
+U32 = mybir.dt.uint32
+U8 = mybir.dt.uint8
+MULT = mybir.AluOpType.mult
+ADD = mybir.AluOpType.add
+
+P = 128
+TOKENS = 512
+K = 2048
+N = 5632
+FLOPS = 2 * TOKENS * K * N
+
+PASSES = K // 512
+MT = TOKENS // P
+UNIT = 256
+UNITS = N // UNIT
+PIECE = 1024
+PIECES = (N + PIECE - 1) // PIECE
+RAW_BUFS = 8
+GROUP_SIZES = (4, 4, 4, 4, 4, 1, 1)
+VECTOR_EVAC_FROM = UNITS - 1
+
+
+def tile_unicorelinearfp4_kernel(tc, x, weight, wscales, bias, out):
+    nc = tc.nc
+    x_rows = x.flatten_outer_dims().rearrange("(p m) k -> p m k", m=MT)
+    out_rows = out.flatten_outer_dims().rearrange("(p m) n -> p m n", m=MT)
+    ws_vec = wscales.rearrange("n o -> (n o)")
+    bias_vec = bias.rearrange("o n -> (o n)")
+
+    group_of = {}
+    group_start = []
+    first = 0
+    for gi, size in enumerate(GROUP_SIZES):
+        group_start.append(first)
+        for u in range(first, first + size):
+            group_of[u] = gi
+        first += size
+    assert first == UNITS
+
+    with ExitStack() as ctx:
+        const = ctx.enter_context(tc.tile_pool(name="const", bufs=1))
+        xg_pool = ctx.enter_context(tc.tile_pool(name="xg", bufs=2))
+        raw_pool = ctx.enter_context(tc.tile_pool(name="raw", bufs=RAW_BUFS))
+        sx_pool = ctx.enter_context(tc.tile_pool(name="sx", bufs=3))
+        grp_pool = ctx.enter_context(tc.tile_pool(name="grp", bufs=2))
+        code_pool = ctx.enter_context(tc.tile_pool(name="code", bufs=3))
+        stage_pool = ctx.enter_context(tc.tile_pool(name="stage", bufs=3))
+        tp_pool = ctx.enter_context(tc.psum_pool(name="tp", bufs=6))
+        acc_pool = ctx.enter_context(tc.psum_pool(name="acc", bufs=2))
+        ctx.enter_context(tc.manual_schedule())
+
+        ident = const.tile([P, P], F32, name="ident")
+        sb = const.tile([P, N], BF16, name="sb")
+        bias_sb = const.tile([P, N], BF16, name="bias_sb")
+        xraw = const.tile([P, MT, K], BF16, name="xraw")
+        xcodes = const.tile([P, MT, PASSES * P], U32, name="xcodes", align_bytes=64)
+        xplane = const.tile([P, MT, PASSES * P], U8, name="xplane", align_bytes=64)
+
+        raw = {}
+        tp = {}
+        sx = {}
+        grp = {}
+        codes = {}
+        plane = {}
+        acc = {}
+        stage = {}
+
+        def load_piece(dst, vec, q):
+            a = q * PIECE
+            b = min(N, a + PIECE)
+            src = vec[a:b].partition_broadcast(P)
+            assert tuple(src.shape) == (P, b - a), "partition_broadcast gave %s" % str(tuple(src.shape))
+            nc.sync.dma_start(out=dst[:, a:b], in_=src)
+
+        def load_unit(i):
+            raw[i] = raw_pool.tile([P, 2, K], BF16, name="raw%d" % i, tag="raw")
+            rows = weight[i * UNIT : (i + 1) * UNIT, :].rearrange("(p j) k -> p j k", j=2)
+            nc.sync.dma_start(out=raw[i][:], in_=rows)
+            if i % 4 == 3 and (i + 1) // 4 < PIECES:
+                load_piece(sb, ws_vec, (i + 1) // 4)
+                load_piece(bias_sb, bias_vec, (i + 1) // 4)
+
+        def expand_scales(i):
+            sx[i] = sx_pool.tile([P, 4 * UNIT], BF16, name="sx%d" % i, tag="sx")
+            nc.scalar.copy(
+                out=sx[i][:].rearrange("p (n r) -> p n r", r=4),
+                in_=sb[:, i * UNIT : (i + 1) * UNIT].unsqueeze(2).to_broadcast([P, UNIT, 4]),
+            )
+
+        def transpose_unit(i):
+            for g in range(PASSES):
+                bank = tp_pool.tile([P, 512], F32, name="tp%d_%d" % (i, g), tag="tp")
+                tp[(i, g)] = bank
+                for j in range(2):
+                    words = raw[i][:, j, :].bitcast(F32)
+                    for h in range(2):
+                        s = 2 * j + h
+                        blk = 2 * g + h
+                        nc.tensor.transpose(
+                            bank[:, s * P : (s + 1) * P],
+                            words[:, blk * P : (blk + 1) * P],
+                            ident[:],
+                        )
+
+        def scale_unit(i, passes):
+            if 0 in passes:
+                grp[i] = grp_pool.tile([P, PASSES * 4 * UNIT], BF16, name="grp%d" % i, tag="grp", align_bytes=64)
+            for g in passes:
+                nc.vector.tensor_tensor(
+                    out=grp[i][:, g * 1024 : (g + 1) * 1024].rearrange("p (c s e) -> p c s e", s=4, e=2),
+                    in0=tp[(i, g)][:].bitcast(BF16).rearrange("p (s c e) -> p c s e", s=4, e=2),
+                    in1=sx[i][:].rearrange("p (c s e) -> p c s e", s=4, e=2),
+                    op=MULT,
+                )
+
+        def quantise_unit(i):
+            codes[i] = code_pool.tile([P, PASSES * UNIT], U32, name="codes%d" % i, tag="codes", align_bytes=64)
+            plane[i] = code_pool.tile([P, PASSES * UNIT], U8, name="plane%d" % i, tag="plane", align_bytes=64)
+            nc.vector.quantize_mx(out=codes[i][:].bitcast(FP8X4), scales=plane[i][:], in_=grp[i][:])
+
+        def multiply_unit(i, b):
+            bank = acc_pool.tile([P, 512], F32, name="acc%d_%d" % (i, b), tag="acc")
+            acc[(i, b)] = bank
+            for mm in range(2):
+                m = 2 * b + mm
+                for g in range(PASSES):
+                    nc.tensor.matmul_mx(
+                        out=bank[:, mm * UNIT : (mm + 1) * UNIT],
+                        lhsT=xcodes[:, m, g * P : (g + 1) * P].bitcast(FP8X4),
+                        lhsT_scale=xplane[:, m, g * P : (g + 1) * P],
+                        rhs=codes[i][:, g * UNIT : (g + 1) * UNIT].bitcast(FP8X4),
+                        rhs_scale=plane[i][:, g * UNIT : (g + 1) * UNIT],
+                        start=(g == 0),
+                        stop=(g == PASSES - 1),
+                    )
+
+        def finish_unit(i):
+            gi = group_of[i]
+            if i == group_start[gi]:
+                stage[gi] = stage_pool.tile([P, MT, 4 * UNIT], F32, name="stage%d" % gi, tag="stage")
+            off = (i - group_start[gi]) * UNIT
+            for b in range(2):
+                dst = stage[gi][:, 2 * b : 2 * b + 2, off : off + UNIT]
+                src = acc[(i, b)][:].rearrange("p (m n) -> p m n", m=2)
+                row = bias_sb[:, i * UNIT : (i + 1) * UNIT].unsqueeze(1).to_broadcast([P, 2, UNIT])
+                if i >= VECTOR_EVAC_FROM:
+                    nc.vector.tensor_tensor(out=dst, in0=src, in1=row, op=ADD)
+                else:
+                    nc.scalar.copy(out=dst, in_=src)
+                    nc.gpsimd.tensor_tensor(out=dst, in0=dst, in1=row, op=ADD)
+            if i == group_start[gi] + GROUP_SIZES[gi] - 1:
+                a = group_start[gi] * UNIT
+                w = GROUP_SIZES[gi] * UNIT
+                nc.sync.dma_start(out=out_rows[:, :, a : a + w], in_=stage[gi][:, :, 0:w])
+
+        def prepare_x(m):
+            xg = xg_pool.tile([P, PASSES * 4 * P], BF16, name="xg%d" % m, tag="xg", align_bytes=64)
+            words = xraw[:, m, :].bitcast(F32)
+            for b in range(2):
+                bank = tp_pool.tile([P, 512], F32, name="tpx%d_%d" % (m, b), tag="tp")
+                for s in range(4):
+                    blk = 4 * b + s
+                    nc.tensor.transpose(
+                        bank[:, s * P : (s + 1) * P], words[:, blk * P : (blk + 1) * P], ident[:]
+                    )
+                nc.scalar.copy(
+                    out=xg[:, b * 1024 : (b + 1) * 1024].bitcast(F32).rearrange("p (g c h) -> p g c h", g=2, h=2),
+                    in_=bank[:].rearrange("p (g h c) -> p g c h", g=2, h=2),
+                )
+            nc.vector.quantize_mx(out=xcodes[:, m, :].bitcast(FP8X4), scales=xplane[:, m, :], in_=xg[:])
+
+        make_identity(nc, ident[:])
+        load_piece(sb, ws_vec, 0)
+        load_unit(0)
+        for m in range(MT):
+            nc.sync.dma_start(out=xraw[:, m, :], in_=x_rows[:, m, :])
+        load_unit(1)
+        load_piece(bias_sb, bias_vec, 0)
+        for i in range(2, RAW_BUFS):
+            load_unit(i)
+
+        expand_scales(0)
+        expand_scales(1)
+        transpose_unit(0)
+        scale_unit(0, (0, 1, 2, 3))
+        prepare_x(0)
+        quantise_unit(0)
+        for m in range(1, MT):
+            prepare_x(m)
+        transpose_unit(1)
+        next_t = 2
+        next_load = RAW_BUFS
+        for k in range(UNITS + 1):
+            if k + 2 < UNITS:
+                expand_scales(k + 2)
+            if k + 1 < UNITS:
+                scale_unit(k + 1, (0,))
+            if 1 <= k < UNITS:
+                quantise_unit(k)
+            if k < UNITS:
+                multiply_unit(k, 0)
+                multiply_unit(k, 1)
+                for t in range(2 if k == 0 else 1):
+                    if next_t < UNITS:
+                        transpose_unit(next_t)
+                        while next_load < UNITS and next_load <= next_t + RAW_BUFS:
+                            load_unit(next_load)
+                            next_load += 1
+                        next_t += 1
+            if k + 1 < UNITS:
+                scale_unit(k + 1, (1, 2, 3))
+            if k >= 1:
+                finish_unit(k - 1)

@@ -8,6 +8,7 @@ BF16 = mybir.dt.bfloat16
 F32 = mybir.dt.float32
 U32 = mybir.dt.uint32
 U8 = mybir.dt.uint8
+I32 = mybir.dt.int32
 MULT = mybir.AluOpType.mult
 ADD = mybir.AluOpType.add
 
@@ -22,6 +23,7 @@ MT = TOKENS // P
 UNIT = 256
 UNITS = N // UNIT
 PIECE = 1024
+BIAS_ROW = 32
 PIECES = (N + PIECE - 1) // PIECE
 RAW_BUFS = 8
 GROUP_SIZES = (4, 4, 4, 4, 4, 1, 1)
@@ -58,6 +60,8 @@ def tile_unicorelinearfp4_kernel(tc, x, weight, wscales, bias, out):
         ctx.enter_context(tc.manual_schedule())
 
         ident = const.tile([P, P], F32, name="ident")
+        vrows = const.tile([P, UNIT], BF16, name="vrows")
+        pv = const.tile([P, P], F32, name="pv")
         sb = const.tile([P, N], BF16, name="sb")
         bias_sb = const.tile([P, N], BF16, name="bias_sb")
         xraw = const.tile([P, MT, K], BF16, name="xraw")
@@ -73,20 +77,24 @@ def tile_unicorelinearfp4_kernel(tc, x, weight, wscales, bias, out):
         acc = {}
         stage = {}
 
-        def load_piece(dst, vec, q):
-            a = q * PIECE
-            b = min(N, a + PIECE)
-            src = vec[a:b].partition_broadcast(P)
-            assert tuple(src.shape) == (P, b - a), "partition_broadcast gave %s" % str(tuple(src.shape))
-            nc.sync.dma_start(out=dst[:, a:b], in_=src)
+        def spread(dst, row0, q, on_vector):
+            units = min(4, UNITS - 4 * q)
+            bank = acc_pool.tile([P, 512], F32, name="sp%d_%d" % (row0, q), tag="acc")
+            for u in range(units):
+                r = row0 + 4 * q + u
+                nc.tensor.transpose(
+                    bank[:, u * P : (u + 1) * P], pv[:, r : r + 1].to_broadcast([P, P]), ident[:]
+                )
+            words = dst[:, q * PIECE : q * PIECE + units * UNIT].bitcast(F32)
+            if on_vector:
+                nc.vector.tensor_copy(out=words, in_=bank[:, 0 : units * P])
+            else:
+                nc.scalar.copy(out=words, in_=bank[:, 0 : units * P])
 
         def load_unit(i):
             raw[i] = raw_pool.tile([P, 2, K], BF16, name="raw%d" % i, tag="raw")
             rows = weight[i * UNIT : (i + 1) * UNIT, :].rearrange("(p j) k -> p j k", j=2)
             nc.sync.dma_start(out=raw[i][:], in_=rows)
-            if i % 4 == 3 and (i + 1) // 4 < PIECES:
-                load_piece(sb, ws_vec, (i + 1) // 4)
-                load_piece(bias_sb, bias_vec, (i + 1) // 4)
 
         def expand_scales(i):
             sx[i] = sx_pool.tile([P, 4 * UNIT], BF16, name="sx%d" % i, tag="sx")
@@ -178,17 +186,31 @@ def tile_unicorelinearfp4_kernel(tc, x, weight, wscales, bias, out):
             nc.vector.quantize_mx(out=xcodes[:, m, :].bitcast(FP8X4), scales=xplane[:, m, :], in_=xg[:])
 
         make_identity(nc, ident[:])
-        load_piece(sb, ws_vec, 0)
+        nc.vector.memset(vrows[:].bitcast(I32), 0)
+        nc.sync.dma_start(out=vrows[0:UNITS, :], in_=ws_vec.rearrange("(r n) -> r n", n=UNIT))
+        nc.sync.dma_start(
+            out=vrows[BIAS_ROW : BIAS_ROW + UNITS, :], in_=bias_vec.rearrange("(r n) -> r n", n=UNIT)
+        )
         load_unit(0)
         for m in range(MT):
             nc.sync.dma_start(out=xraw[:, m, :], in_=x_rows[:, m, :])
-        load_unit(1)
-        load_piece(bias_sb, bias_vec, 0)
-        for i in range(2, RAW_BUFS):
+        for i in range(1, RAW_BUFS):
             load_unit(i)
 
+        pv_bank = acc_pool.tile([P, 512], F32, name="pv_bank", tag="acc")
+        nc.tensor.transpose(pv_bank[:, 0:P], vrows[:].bitcast(F32), ident[:])
+        nc.vector.tensor_copy(out=pv[:], in_=pv_bank[:, 0:P])
+        spread(sb, 0, 0, False)
         expand_scales(0)
         expand_scales(1)
+        spread(bias_sb, BIAS_ROW, 0, True)
+        spread(sb, 0, 1, True)
+        later = []
+        for q in range(1, PIECES):
+            later.append((bias_sb, BIAS_ROW, q))
+            if q + 1 < PIECES:
+                later.append((sb, 0, q + 1))
+
         transpose_unit(0)
         scale_unit(0, (0, 1, 2, 3))
         prepare_x(0)
@@ -205,6 +227,11 @@ def tile_unicorelinearfp4_kernel(tc, x, weight, wscales, bias, out):
                 scale_unit(k + 1, (0,))
             if 1 <= k < UNITS:
                 quantise_unit(k)
+            if k >= 1:
+                finish_unit(k - 1)
+                if k - 1 < len(later):
+                    dst, row0, q = later[k - 1]
+                    spread(dst, row0, q, False)
             if k < UNITS:
                 multiply_unit(k, 0)
                 multiply_unit(k, 1)
@@ -217,5 +244,3 @@ def tile_unicorelinearfp4_kernel(tc, x, weight, wscales, bias, out):
                         next_t += 1
             if k + 1 < UNITS:
                 scale_unit(k + 1, (1, 2, 3))
-            if k >= 1:
-                finish_unit(k - 1)

@@ -23,11 +23,10 @@ MT = TOKENS // P
 UNIT = 256
 UNITS = N // UNIT
 PIECE = 1024
-BIAS_ROW = 32
 PIECES = (N + PIECE - 1) // PIECE
-RAW_BUFS = 8
-GROUP_SIZES = (4, 4, 4, 4, 4, 1, 1)
-VECTOR_EVAC_FROM = UNITS - 1
+BIAS_ROW = 32
+RAW_BUFS = 7
+GROUP_SIZES = (4, 4, 4, 4, 2, 2, 1, 1)
 
 
 def tile_unicorelinearfp4_kernel(tc, x, weight, wscales, bias, out):
@@ -51,41 +50,41 @@ def tile_unicorelinearfp4_kernel(tc, x, weight, wscales, bias, out):
         const = ctx.enter_context(tc.tile_pool(name="const", bufs=1))
         xg_pool = ctx.enter_context(tc.tile_pool(name="xg", bufs=2))
         raw_pool = ctx.enter_context(tc.tile_pool(name="raw", bufs=RAW_BUFS))
-        sx_pool = ctx.enter_context(tc.tile_pool(name="sx", bufs=3))
-        grp_pool = ctx.enter_context(tc.tile_pool(name="grp", bufs=2))
-        code_pool = ctx.enter_context(tc.tile_pool(name="code", bufs=3))
+        scl_pool = ctx.enter_context(tc.tile_pool(name="scl", bufs=3))
+        grp_pool = ctx.enter_context(tc.tile_pool(name="grp", bufs=3))
+        code_pool = ctx.enter_context(tc.tile_pool(name="code", bufs=4))
         stage_pool = ctx.enter_context(tc.tile_pool(name="stage", bufs=3))
-        tp_pool = ctx.enter_context(tc.psum_pool(name="tp", bufs=6))
-        acc_pool = ctx.enter_context(tc.psum_pool(name="acc", bufs=2))
+        tp_pool = ctx.enter_context(tc.psum_pool(name="tp", bufs=4))
+        acc_pool = ctx.enter_context(tc.psum_pool(name="acc", bufs=4))
         ctx.enter_context(tc.manual_schedule())
 
         ident = const.tile([P, P], F32, name="ident")
         vrows = const.tile([P, UNIT], BF16, name="vrows")
         pv = const.tile([P, P], F32, name="pv")
-        sb = const.tile([P, N], BF16, name="sb")
         bias_sb = const.tile([P, N], BF16, name="bias_sb")
         xraw = const.tile([P, MT, K], BF16, name="xraw")
         xcodes = const.tile([P, MT, PASSES * P], U32, name="xcodes", align_bytes=64)
         xplane = const.tile([P, MT, PASSES * P], U8, name="xplane", align_bytes=64)
+        ws_pp = pv[:, 0:UNITS].bitcast(BF16)
 
         raw = {}
+        scl = {}
         tp = {}
-        sx = {}
         grp = {}
         codes = {}
         plane = {}
         acc = {}
         stage = {}
 
-        def spread(dst, row0, q, on_vector):
+        def spread_bias(q, on_vector):
             units = min(4, UNITS - 4 * q)
-            bank = acc_pool.tile([P, 512], F32, name="sp%d_%d" % (row0, q), tag="acc")
+            bank = acc_pool.tile([P, 512], F32, name="sp%d" % q, tag="acc")
             for u in range(units):
-                r = row0 + 4 * q + u
+                r = BIAS_ROW + 4 * q + u
                 nc.tensor.transpose(
                     bank[:, u * P : (u + 1) * P], pv[:, r : r + 1].to_broadcast([P, P]), ident[:]
                 )
-            words = dst[:, q * PIECE : q * PIECE + units * UNIT].bitcast(F32)
+            words = bias_sb[:, q * PIECE : q * PIECE + units * UNIT].bitcast(F32)
             if on_vector:
                 nc.vector.tensor_copy(out=words, in_=bank[:, 0 : units * P])
             else:
@@ -96,19 +95,23 @@ def tile_unicorelinearfp4_kernel(tc, x, weight, wscales, bias, out):
             rows = weight[i * UNIT : (i + 1) * UNIT, :].rearrange("(p j) k -> p j k", j=2)
             nc.sync.dma_start(out=raw[i][:], in_=rows)
 
-        def expand_scales(i):
-            sx[i] = sx_pool.tile([P, 4 * UNIT], BF16, name="sx%d" % i, tag="sx")
-            nc.scalar.copy(
-                out=sx[i][:].rearrange("p (n r) -> p n r", r=4),
-                in_=sb[:, i * UNIT : (i + 1) * UNIT].unsqueeze(2).to_broadcast([P, UNIT, 4]),
-            )
+        def prescale_unit(i):
+            scl[i] = scl_pool.tile([P, 2, K], BF16, name="scl%d" % i, tag="scl")
+            for j in range(2):
+                nc.vector.tensor_scalar(
+                    out=scl[i][:, j, :],
+                    in0=raw[i][:, j, :],
+                    scalar1=ws_pp[:, 2 * i + j : 2 * i + j + 1],
+                    scalar2=None,
+                    op0=MULT,
+                )
 
         def transpose_unit(i):
+            grp[i] = grp_pool.tile([P, PASSES * 4 * UNIT], BF16, name="grp%d" % i, tag="grp", align_bytes=64)
             for g in range(PASSES):
                 bank = tp_pool.tile([P, 512], F32, name="tp%d_%d" % (i, g), tag="tp")
-                tp[(i, g)] = bank
                 for j in range(2):
-                    words = raw[i][:, j, :].bitcast(F32)
+                    words = scl[i][:, j, :].bitcast(F32)
                     for h in range(2):
                         s = 2 * j + h
                         blk = 2 * g + h
@@ -117,16 +120,9 @@ def tile_unicorelinearfp4_kernel(tc, x, weight, wscales, bias, out):
                             words[:, blk * P : (blk + 1) * P],
                             ident[:],
                         )
-
-        def scale_unit(i, passes):
-            if 0 in passes:
-                grp[i] = grp_pool.tile([P, PASSES * 4 * UNIT], BF16, name="grp%d" % i, tag="grp", align_bytes=64)
-            for g in passes:
-                nc.vector.tensor_tensor(
-                    out=grp[i][:, g * 1024 : (g + 1) * 1024].rearrange("p (c s e) -> p c s e", s=4, e=2),
-                    in0=tp[(i, g)][:].bitcast(BF16).rearrange("p (s c e) -> p c s e", s=4, e=2),
-                    in1=sx[i][:].rearrange("p (c s e) -> p c s e", s=4, e=2),
-                    op=MULT,
+                nc.scalar.copy(
+                    out=grp[i][:, g * 1024 : (g + 1) * 1024].bitcast(F32).rearrange("p (c s) -> p c s", s=4),
+                    in_=bank[:].rearrange("p (s c) -> p c s", s=4),
                 )
 
         def quantise_unit(i):
@@ -155,15 +151,14 @@ def tile_unicorelinearfp4_kernel(tc, x, weight, wscales, bias, out):
             if i == group_start[gi]:
                 stage[gi] = stage_pool.tile([P, MT, 4 * UNIT], F32, name="stage%d" % gi, tag="stage")
             off = (i - group_start[gi]) * UNIT
+            row = bias_sb[:, i * UNIT : (i + 1) * UNIT].unsqueeze(1).to_broadcast([P, 2, UNIT])
             for b in range(2):
-                dst = stage[gi][:, 2 * b : 2 * b + 2, off : off + UNIT]
-                src = acc[(i, b)][:].rearrange("p (m n) -> p m n", m=2)
-                row = bias_sb[:, i * UNIT : (i + 1) * UNIT].unsqueeze(1).to_broadcast([P, 2, UNIT])
-                if i >= VECTOR_EVAC_FROM:
-                    nc.vector.tensor_tensor(out=dst, in0=src, in1=row, op=ADD)
-                else:
-                    nc.scalar.copy(out=dst, in_=src)
-                    nc.gpsimd.tensor_tensor(out=dst, in0=dst, in1=row, op=ADD)
+                nc.vector.tensor_tensor(
+                    out=stage[gi][:, 2 * b : 2 * b + 2, off : off + UNIT],
+                    in0=acc[(i, b)][:].rearrange("p (m n) -> p m n", m=2),
+                    in1=row,
+                    op=ADD,
+                )
             if i == group_start[gi] + GROUP_SIZES[gi] - 1:
                 a = group_start[gi] * UNIT
                 w = GROUP_SIZES[gi] * UNIT
@@ -200,47 +195,45 @@ def tile_unicorelinearfp4_kernel(tc, x, weight, wscales, bias, out):
         pv_bank = acc_pool.tile([P, 512], F32, name="pv_bank", tag="acc")
         nc.tensor.transpose(pv_bank[:, 0:P], vrows[:].bitcast(F32), ident[:])
         nc.vector.tensor_copy(out=pv[:], in_=pv_bank[:, 0:P])
-        spread(sb, 0, 0, False)
-        expand_scales(0)
-        expand_scales(1)
-        spread(bias_sb, BIAS_ROW, 0, True)
-        spread(sb, 0, 1, True)
-        later = []
-        for q in range(1, PIECES):
-            later.append((bias_sb, BIAS_ROW, q))
-            if q + 1 < PIECES:
-                later.append((sb, 0, q + 1))
+        spread_bias(0, True)
 
-        transpose_unit(0)
-        scale_unit(0, (0, 1, 2, 3))
+        state = {"ps": 0, "t": 0, "q": 0, "load": RAW_BUFS, "piece": 1}
+
+        def next_prescale():
+            prescale_unit(state["ps"])
+            if state["load"] < UNITS:
+                load_unit(state["load"])
+                state["load"] += 1
+            state["ps"] += 1
+
+        def next_transpose():
+            while state["ps"] <= state["t"]:
+                next_prescale()
+            transpose_unit(state["t"])
+            state["t"] += 1
+
+        def next_quantise():
+            quantise_unit(state["q"])
+            state["q"] += 1
+
+        next_transpose()
         prepare_x(0)
-        quantise_unit(0)
+        next_quantise()
         for m in range(1, MT):
             prepare_x(m)
-        transpose_unit(1)
-        next_t = 2
-        next_load = RAW_BUFS
         for k in range(UNITS + 1):
-            if k + 2 < UNITS:
-                expand_scales(k + 2)
-            if k + 1 < UNITS:
-                scale_unit(k + 1, (0,))
-            if 1 <= k < UNITS:
-                quantise_unit(k)
+            lead = 2 if k == 0 else k + 3
+            while state["t"] < min(UNITS, lead):
+                next_transpose()
+            while state["ps"] < min(UNITS, state["t"] + 1):
+                next_prescale()
             if k >= 1:
                 finish_unit(k - 1)
-                if k - 1 < len(later):
-                    dst, row0, q = later[k - 1]
-                    spread(dst, row0, q, False)
+            while state["q"] < min(UNITS, state["t"], k + 3):
+                next_quantise()
+            if k % 2 == 1 and state["piece"] < PIECES:
+                spread_bias(state["piece"], False)
+                state["piece"] += 1
             if k < UNITS:
                 multiply_unit(k, 0)
                 multiply_unit(k, 1)
-                for t in range(2 if k == 0 else 1):
-                    if next_t < UNITS:
-                        transpose_unit(next_t)
-                        while next_load < UNITS and next_load <= next_t + RAW_BUFS:
-                            load_unit(next_load)
-                            next_load += 1
-                        next_t += 1
-            if k + 1 < UNITS:
-                scale_unit(k + 1, (1, 2, 3))

@@ -159,7 +159,12 @@ def tile_unicorelinearfp4_kernel(tc, x, weight, wscales, bias, out):
                     in1=row,
                     op=ADD,
                 )
-            if i == group_start[gi] + GROUP_SIZES[gi] - 1:
+                if i == UNITS - 1:
+                    nc.sync.dma_start(
+                        out=out_rows[:, 2 * b : 2 * b + 2, i * UNIT : (i + 1) * UNIT],
+                        in_=stage[gi][:, 2 * b : 2 * b + 2, off : off + UNIT],
+                    )
+            if i == group_start[gi] + GROUP_SIZES[gi] - 1 and i < UNITS - 1:
                 a = group_start[gi] * UNIT
                 w = GROUP_SIZES[gi] * UNIT
                 nc.sync.dma_start(out=out_rows[:, :, a : a + w], in_=stage[gi][:, :, 0:w])
@@ -195,9 +200,10 @@ def tile_unicorelinearfp4_kernel(tc, x, weight, wscales, bias, out):
         pv_bank = acc_pool.tile([P, 512], F32, name="pv_bank", tag="acc")
         nc.tensor.transpose(pv_bank[:, 0:P], vrows[:].bitcast(F32), ident[:])
         nc.vector.tensor_copy(out=pv[:], in_=pv_bank[:, 0:P])
-        spread_bias(0, True)
+        for q in range(PIECES):
+            spread_bias(q, False)
 
-        state = {"ps": 0, "t": 0, "q": 0, "load": RAW_BUFS, "piece": 1}
+        state = {"ps": 0, "t": 0, "q": 0, "load": RAW_BUFS}
 
         def next_prescale():
             prescale_unit(state["ps"])
@@ -221,6 +227,7 @@ def tile_unicorelinearfp4_kernel(tc, x, weight, wscales, bias, out):
         next_quantise()
         for m in range(1, MT):
             prepare_x(m)
+        multiply_unit(0, 0)
         for k in range(UNITS + 1):
             lead = 2 if k == 0 else k + 3
             while state["t"] < min(UNITS, lead):
@@ -231,9 +238,7 @@ def tile_unicorelinearfp4_kernel(tc, x, weight, wscales, bias, out):
                 finish_unit(k - 1)
             while state["q"] < min(UNITS, state["t"], k + 3):
                 next_quantise()
-            if k % 2 == 1 and state["piece"] < PIECES:
-                spread_bias(state["piece"], False)
-                state["piece"] += 1
             if k < UNITS:
-                multiply_unit(k, 0)
+                if k > 0:
+                    multiply_unit(k, 0)
                 multiply_unit(k, 1)

@@ -54,8 +54,8 @@ def tile_unicorelinearfp4_kernel(tc, x, weight, wscales, bias, out):
         grp_pool = ctx.enter_context(tc.tile_pool(name="grp", bufs=3))
         code_pool = ctx.enter_context(tc.tile_pool(name="code", bufs=4))
         stage_pool = ctx.enter_context(tc.tile_pool(name="stage", bufs=3))
-        tp_pool = ctx.enter_context(tc.psum_pool(name="tp", bufs=4))
-        acc_pool = ctx.enter_context(tc.psum_pool(name="acc", bufs=4))
+        tp_pool = ctx.enter_context(tc.psum_pool(name="tp", bufs=5))
+        acc_pool = ctx.enter_context(tc.psum_pool(name="acc", bufs=3))
         ctx.enter_context(tc.manual_schedule())
 
         ident = const.tile([P, P], F32, name="ident")
@@ -169,8 +169,10 @@ def tile_unicorelinearfp4_kernel(tc, x, weight, wscales, bias, out):
                 w = GROUP_SIZES[gi] * UNIT
                 nc.sync.dma_start(out=out_rows[:, :, a : a + w], in_=stage[gi][:, :, 0:w])
 
-        def prepare_x(m):
-            xg = xg_pool.tile([P, PASSES * 4 * P], BF16, name="xg%d" % m, tag="xg", align_bytes=64)
+        xg = {}
+
+        def transpose_x(m, second_on_vector):
+            xg[m] = xg_pool.tile([P, PASSES * 4 * P], BF16, name="xg%d" % m, tag="xg", align_bytes=64)
             words = xraw[:, m, :].bitcast(F32)
             for b in range(2):
                 bank = tp_pool.tile([P, 512], F32, name="tpx%d_%d" % (m, b), tag="tp")
@@ -179,11 +181,15 @@ def tile_unicorelinearfp4_kernel(tc, x, weight, wscales, bias, out):
                     nc.tensor.transpose(
                         bank[:, s * P : (s + 1) * P], words[:, blk * P : (blk + 1) * P], ident[:]
                     )
-                nc.scalar.copy(
-                    out=xg[:, b * 1024 : (b + 1) * 1024].bitcast(F32).rearrange("p (g c h) -> p g c h", g=2, h=2),
-                    in_=bank[:].rearrange("p (g h c) -> p g c h", g=2, h=2),
-                )
-            nc.vector.quantize_mx(out=xcodes[:, m, :].bitcast(FP8X4), scales=xplane[:, m, :], in_=xg[:])
+                dst = xg[m][:, b * 1024 : (b + 1) * 1024].bitcast(F32).rearrange("p (g c h) -> p g c h", g=2, h=2)
+                src = bank[:].rearrange("p (g h c) -> p g c h", g=2, h=2)
+                if b == 1 and second_on_vector:
+                    nc.vector.tensor_copy(out=dst, in_=src)
+                else:
+                    nc.scalar.copy(out=dst, in_=src)
+
+        def quantise_x(m):
+            nc.vector.quantize_mx(out=xcodes[:, m, :].bitcast(FP8X4), scales=xplane[:, m, :], in_=xg[m][:])
 
         make_identity(nc, ident[:])
         nc.vector.memset(vrows[:].bitcast(I32), 0)
@@ -201,7 +207,7 @@ def tile_unicorelinearfp4_kernel(tc, x, weight, wscales, bias, out):
         nc.tensor.transpose(pv_bank[:, 0:P], vrows[:].bitcast(F32), ident[:])
         nc.vector.tensor_copy(out=pv[:], in_=pv_bank[:, 0:P])
         for q in range(PIECES):
-            spread_bias(q, False)
+            spread_bias(q, q == 1)
 
         state = {"ps": 0, "t": 0, "q": 0, "load": RAW_BUFS}
 
@@ -223,22 +229,43 @@ def tile_unicorelinearfp4_kernel(tc, x, weight, wscales, bias, out):
             state["q"] += 1
 
         next_transpose()
-        prepare_x(0)
+        transpose_x(0, True)
         next_quantise()
-        for m in range(1, MT):
-            prepare_x(m)
+        transpose_x(1, True)
+        quantise_x(0)
+        quantise_x(1)
+        next_prescale()
+        transpose_x(2, False)
+        quantise_x(2)
+        transpose_x(3, False)
+        quantise_x(3)
+        next_prescale()
         multiply_unit(0, 0)
-        for k in range(UNITS + 1):
-            lead = 2 if k == 0 else k + 3
-            while state["t"] < min(UNITS, lead):
+        next_transpose()
+        multiply_unit(0, 1)
+
+        next_transpose()
+        next_quantise()
+        next_transpose()
+        finish_unit(0)
+        multiply_unit(1, 0)
+        multiply_unit(1, 1)
+        next_prescale()
+        next_prescale()
+        for a in range(2, UNITS, 2):
+            next_quantise()
+            if a + 2 < UNITS:
                 next_transpose()
-            while state["ps"] < min(UNITS, state["t"] + 1):
+            finish_unit(a - 1)
+            next_quantise()
+            if a + 3 < UNITS:
+                next_transpose()
+            for i in (a, a + 1):
+                multiply_unit(i, 0)
+                multiply_unit(i, 1)
+            if state["ps"] < UNITS:
                 next_prescale()
-            if k >= 1:
-                finish_unit(k - 1)
-            while state["q"] < min(UNITS, state["t"], k + 3):
-                next_quantise()
-            if k < UNITS:
-                if k > 0:
-                    multiply_unit(k, 0)
-                multiply_unit(k, 1)
+            finish_unit(a)
+            if state["ps"] < UNITS:
+                next_prescale()
+        finish_unit(UNITS - 1)

@@ -54,8 +54,8 @@ def tile_unicorelinearfp4_kernel(tc, x, weight, wscales, bias, out):
         grp_pool = ctx.enter_context(tc.tile_pool(name="grp", bufs=3))
         code_pool = ctx.enter_context(tc.tile_pool(name="code", bufs=4))
         stage_pool = ctx.enter_context(tc.tile_pool(name="stage", bufs=3))
-        tp_pool = ctx.enter_context(tc.psum_pool(name="tp", bufs=5))
-        acc_pool = ctx.enter_context(tc.psum_pool(name="acc", bufs=3))
+        tp_pool = ctx.enter_context(tc.psum_pool(name="tp", bufs=4))
+        acc_pool = ctx.enter_context(tc.psum_pool(name="acc", bufs=4))
         ctx.enter_context(tc.manual_schedule())
 
         ident = const.tile([P, P], F32, name="ident")
@@ -241,31 +241,17 @@ def tile_unicorelinearfp4_kernel(tc, x, weight, wscales, bias, out):
         quantise_x(3)
         next_prescale()
         multiply_unit(0, 0)
-        next_transpose()
-        multiply_unit(0, 1)
-
-        next_transpose()
-        next_quantise()
-        next_transpose()
-        finish_unit(0)
-        multiply_unit(1, 0)
-        multiply_unit(1, 1)
-        next_prescale()
-        next_prescale()
-        for a in range(2, UNITS, 2):
-            next_quantise()
-            if a + 2 < UNITS:
+        for k in range(UNITS + 1):
+            lead = 2 if k == 0 else k + 3
+            while state["t"] < min(UNITS, lead):
                 next_transpose()
-            finish_unit(a - 1)
-            next_quantise()
-            if a + 3 < UNITS:
-                next_transpose()
-            for i in (a, a + 1):
-                multiply_unit(i, 0)
-                multiply_unit(i, 1)
-            if state["ps"] < UNITS:
+            while state["ps"] < min(UNITS, state["t"] + 1):
                 next_prescale()
-            finish_unit(a)
-            if state["ps"] < UNITS:
-                next_prescale()
-        finish_unit(UNITS - 1)
+            if k >= 1:
+                finish_unit(k - 1)
+            while state["q"] < min(UNITS, state["t"], k + 3):
+                next_quantise()
+            if k < UNITS:
+                if k > 0:
+                    multiply_unit(k, 0)
+                multiply_unit(k, 1)

from contextlib import ExitStack

import concourse.mybir as mybir
from concourse.masks import make_identity

FP8X4 = mybir.dt.float8_e4m3fn_x4
BF16 = mybir.dt.bfloat16
F32 = mybir.dt.float32
U32 = mybir.dt.uint32
U8 = mybir.dt.uint8
I32 = mybir.dt.int32
MULT = mybir.AluOpType.mult
ADD = mybir.AluOpType.add

P = 128
TOKENS = 512
K = 2048
N = 5632
FLOPS = 2 * TOKENS * K * N

PASSES = K // 512
MT = TOKENS // P
UNIT = 256
UNITS = N // UNIT
PIECE = 1024
PIECES = (N + PIECE - 1) // PIECE
BIAS_ROW = 32
RAW_BUFS = 7
GROUP_SIZES = (4, 4, 4, 4, 2, 2, 1, 1)


def tile_unicorelinearfp4_kernel(tc, x, weight, wscales, bias, out):
    nc = tc.nc
    x_rows = x.flatten_outer_dims().rearrange("(p m) k -> p m k", m=MT)
    out_rows = out.flatten_outer_dims().rearrange("(p m) n -> p m n", m=MT)
    ws_vec = wscales.rearrange("n o -> (n o)")
    bias_vec = bias.rearrange("o n -> (o n)")

    group_of = {}
    group_start = []
    first = 0
    for gi, size in enumerate(GROUP_SIZES):
        group_start.append(first)
        for u in range(first, first + size):
            group_of[u] = gi
        first += size
    assert first == UNITS

    with ExitStack() as ctx:
        const = ctx.enter_context(tc.tile_pool(name="const", bufs=1))
        xg_pool = ctx.enter_context(tc.tile_pool(name="xg", bufs=2))
        raw_pool = ctx.enter_context(tc.tile_pool(name="raw", bufs=RAW_BUFS))
        scl_pool = ctx.enter_context(tc.tile_pool(name="scl", bufs=3))
        grp_pool = ctx.enter_context(tc.tile_pool(name="grp", bufs=3))
        code_pool = ctx.enter_context(tc.tile_pool(name="code", bufs=4))
        stage_pool = ctx.enter_context(tc.tile_pool(name="stage", bufs=3))
        tp_pool = ctx.enter_context(tc.psum_pool(name="tp", bufs=4))
        acc_pool = ctx.enter_context(tc.psum_pool(name="acc", bufs=4))
        ctx.enter_context(tc.manual_schedule())

        ident = const.tile([P, P], F32, name="ident")
        vrows = const.tile([P, UNIT], BF16, name="vrows")
        pv = const.tile([P, P], F32, name="pv")
        bias_sb = const.tile([P, N], BF16, name="bias_sb")
        xraw = const.tile([P, MT, K], BF16, name="xraw")
        xcodes = const.tile([P, MT, PASSES * P], U32, name="xcodes", align_bytes=64)
        xplane = const.tile([P, MT, PASSES * P], U8, name="xplane", align_bytes=64)
        ws_pp = pv[:, 0:UNITS].bitcast(BF16)

        raw = {}
        scl = {}
        tp = {}
        grp = {}
        codes = {}
        plane = {}
        acc = {}
        stage = {}

        def spread_bias(q, on_vector):
            units = min(4, UNITS - 4 * q)
            bank = acc_pool.tile([P, 512], F32, name="sp%d" % q, tag="acc")
            for u in range(units):
                r = BIAS_ROW + 4 * q + u
                nc.tensor.transpose(
                    bank[:, u * P : (u + 1) * P], pv[:, r : r + 1].to_broadcast([P, P]), ident[:]
                )
            words = bias_sb[:, q * PIECE : q * PIECE + units * UNIT].bitcast(F32)
            if on_vector:
                nc.vector.tensor_copy(out=words, in_=bank[:, 0 : units * P])
            else:
                nc.scalar.copy(out=words, in_=bank[:, 0 : units * P])

        def load_unit(i):
            raw[i] = raw_pool.tile([P, 2, K], BF16, name="raw%d" % i, tag="raw")
            rows = weight[i * UNIT : (i + 1) * UNIT, :].rearrange("(p j) k -> p j k", j=2)
            nc.sync.dma_start(out=raw[i][:], in_=rows)

        def prescale_unit(i):
            scl[i] = scl_pool.tile([P, 2, K], BF16, name="scl%d" % i, tag="scl")
            for j in range(2):
                nc.vector.tensor_scalar(
                    out=scl[i][:, j, :],
                    in0=raw[i][:, j, :],
                    scalar1=ws_pp[:, 2 * i + j : 2 * i + j + 1],
                    scalar2=None,
                    op0=MULT,
                )

        def transpose_unit(i):
            grp[i] = grp_pool.tile([P, PASSES * 4 * UNIT], BF16, name="grp%d" % i, tag="grp", align_bytes=64)
            for g in range(PASSES):
                bank = tp_pool.tile([P, 512], F32, name="tp%d_%d" % (i, g), tag="tp")
                for j in range(2):
                    words = scl[i][:, j, :].bitcast(F32)
                    for h in range(2):
                        s = 2 * j + h
                        blk = 2 * g + h
                        nc.tensor.transpose(
                            bank[:, s * P : (s + 1) * P],
                            words[:, blk * P : (blk + 1) * P],
                            ident[:],
                        )
                nc.scalar.copy(
                    out=grp[i][:, g * 1024 : (g + 1) * 1024].bitcast(F32).rearrange("p (c s) -> p c s", s=4),
                    in_=bank[:].rearrange("p (s c) -> p c s", s=4),
                )

        def quantise_unit(i):
            codes[i] = code_pool.tile([P, PASSES * UNIT], U32, name="codes%d" % i, tag="codes", align_bytes=64)
            plane[i] = code_pool.tile([P, PASSES * UNIT], U8, name="plane%d" % i, tag="plane", align_bytes=64)
            nc.vector.quantize_mx(out=codes[i][:].bitcast(FP8X4), scales=plane[i][:], in_=grp[i][:])

        def multiply_unit(i, b):
            bank = acc_pool.tile([P, 512], F32, name="acc%d_%d" % (i, b), tag="acc")
            acc[(i, b)] = bank
            for mm in range(2):
                m = 2 * b + mm
                for g in range(PASSES):
                    nc.tensor.matmul_mx(
                        out=bank[:, mm * UNIT : (mm + 1) * UNIT],
                        lhsT=xcodes[:, m, g * P : (g + 1) * P].bitcast(FP8X4),
                        lhsT_scale=xplane[:, m, g * P : (g + 1) * P],
                        rhs=codes[i][:, g * UNIT : (g + 1) * UNIT].bitcast(FP8X4),
                        rhs_scale=plane[i][:, g * UNIT : (g + 1) * UNIT],
                        start=(g == 0),
                        stop=(g == PASSES - 1),
                    )

        def finish_unit(i):
            gi = group_of[i]
            if i == group_start[gi]:
                stage[gi] = stage_pool.tile([P, MT, 4 * UNIT], F32, name="stage%d" % gi, tag="stage")
            off = (i - group_start[gi]) * UNIT
            row = bias_sb[:, i * UNIT : (i + 1) * UNIT].unsqueeze(1).to_broadcast([P, 2, UNIT])
            for b in range(2):
                nc.vector.tensor_tensor(
                    out=stage[gi][:, 2 * b : 2 * b + 2, off : off + UNIT],
                    in0=acc[(i, b)][:].rearrange("p (m n) -> p m n", m=2),
                    in1=row,
                    op=ADD,
                )
                if i == UNITS - 1:
                    nc.sync.dma_start(
                        out=out_rows[:, 2 * b : 2 * b + 2, i * UNIT : (i + 1) * UNIT],
                        in_=stage[gi][:, 2 * b : 2 * b + 2, off : off + UNIT],
                    )
            if i == group_start[gi] + GROUP_SIZES[gi] - 1 and i < UNITS - 1:
                a = group_start[gi] * UNIT
                w = GROUP_SIZES[gi] * UNIT
                nc.sync.dma_start(out=out_rows[:, :, a : a + w], in_=stage[gi][:, :, 0:w])

        xg = {}

        def transpose_x(m, second_on_vector):
            xg[m] = xg_pool.tile([P, PASSES * 4 * P], BF16, name="xg%d" % m, tag="xg", align_bytes=64)
            words = xraw[:, m, :].bitcast(F32)
            for b in range(2):
                bank = tp_pool.tile([P, 512], F32, name="tpx%d_%d" % (m, b), tag="tp")
                for s in range(4):
                    blk = 4 * b + s
                    nc.tensor.transpose(
                        bank[:, s * P : (s + 1) * P], words[:, blk * P : (blk + 1) * P], ident[:]
                    )
                dst = xg[m][:, b * 1024 : (b + 1) * 1024].bitcast(F32).rearrange("p (g c h) -> p g c h", g=2, h=2)
                src = bank[:].rearrange("p (g h c) -> p g c h", g=2, h=2)
                if b == 1 and second_on_vector:
                    nc.vector.tensor_copy(out=dst, in_=src)
                else:
                    nc.scalar.copy(out=dst, in_=src)

        def quantise_x(m):
            nc.vector.quantize_mx(out=xcodes[:, m, :].bitcast(FP8X4), scales=xplane[:, m, :], in_=xg[m][:])

        make_identity(nc, ident[:])
        nc.vector.memset(vrows[:].bitcast(I32), 0)
        nc.sync.dma_start(out=vrows[0:UNITS, :], in_=ws_vec.rearrange("(r n) -> r n", n=UNIT))
        nc.sync.dma_start(
            out=vrows[BIAS_ROW : BIAS_ROW + UNITS, :], in_=bias_vec.rearrange("(r n) -> r n", n=UNIT)
        )
        load_unit(0)
        for m in range(MT):
            nc.sync.dma_start(out=xraw[:, m, :], in_=x_rows[:, m, :])
        for i in range(1, RAW_BUFS):
            load_unit(i)

        pv_bank = acc_pool.tile([P, 512], F32, name="pv_bank", tag="acc")
        nc.tensor.transpose(pv_bank[:, 0:P], vrows[:].bitcast(F32), ident[:])
        nc.vector.tensor_copy(out=pv[:], in_=pv_bank[:, 0:P])
        for q in range(PIECES):
            spread_bias(q, q == 1)

        state = {"ps": 0, "t": 0, "q": 0, "load": RAW_BUFS}

        def next_prescale():
            prescale_unit(state["ps"])
            if state["load"] < UNITS:
                load_unit(state["load"])
                state["load"] += 1
            state["ps"] += 1

        def next_transpose():
            while state["ps"] <= state["t"]:
                next_prescale()
            transpose_unit(state["t"])
            state["t"] += 1

        def next_quantise():
            quantise_unit(state["q"])
            state["q"] += 1

        next_transpose()
        transpose_x(0, True)
        next_quantise()
        transpose_x(1, True)
        quantise_x(0)
        quantise_x(1)
        next_prescale()
        transpose_x(2, False)
        quantise_x(2)
        transpose_x(3, False)
        quantise_x(3)
        next_prescale()
        multiply_unit(0, 0)
        for k in range(UNITS + 1):
            lead = 2 if k == 0 else k + 3
            while state["t"] < min(UNITS, lead):
                next_transpose()
            while state["ps"] < min(UNITS, state["t"] + 1):
                next_prescale()
            if k >= 1:
                finish_unit(k - 1)
            while state["q"] < min(UNITS, state["t"], k + 3):
                next_quantise()
            if k < UNITS:
                if k > 0:
                    multiply_unit(k, 0)
                multiply_unit(k, 1)
